import numpy as np
import ml_dtypes


def mxq(x, axis, fmt="e4m3"):
    dtype, down = {"e4m3": (ml_dtypes.float8_e4m3fn, 7), "e5m2": (ml_dtypes.float8_e5m2, 14)}[fmt]
    v = np.moveaxis(np.asarray(x, np.float32).astype(ml_dtypes.bfloat16).astype(np.float64), axis, -1)
    blocks = v.reshape(v.shape[:-1] + (-1, 32))
    amax = np.abs(blocks).max(-1, keepdims=True)
    byte = np.maximum(np.where(amax > 0, np.frexp(amax)[1] - 1 + 127, 0) - down, 1)
    scale = np.exp2(byte - 127.0)
    codes = (blocks / scale).astype(np.float32).astype(dtype).astype(np.float64)
    return np.moveaxis((codes * scale).reshape(v.shape), -1, axis)


WIDE = False


def mx_kscale(k):
    if not WIDE:
        return np.ones(k)
    levels = np.array([10, -10, 5, -5, 0])
    a = np.random.permutation(np.resize(levels, k // 512 * 4)).reshape(k // 512, 4)
    idx = np.arange(k)
    return np.exp2(a[idx // 512, idx % 128 // 32])


BF16 = ml_dtypes.bfloat16


def bf(x):
    return np.asarray(x, np.float32).astype(BF16)


def f64(x):
    return np.asarray(x).astype(np.float64)


E2M1 = np.array([0.0, 0.5, 1.0, 1.5, 2.0, 3.0, 4.0, 6.0, -0.0, -0.5, -1.0, -1.5, -2.0, -3.0, -4.0, -6.0])


def pack_weight(w, fmt):
    k, n = w.shape
    w = f64(bf(w)).reshape(k // 32, 32, n)
    amax = np.abs(w).max(1)
    if fmt == "e4m3":
        byte = np.frexp(amax)[1] - 1 + 127 - 7
    else:
        mant, ex = np.frexp(amax / 6.0)
        byte = np.where(mant > 0.5, ex, ex - 1) + 127
    byte = np.clip(np.where(amax > 0, byte, 1), 1, 254)
    scaled = (w * np.exp2(127.0 - byte)[:, None, :]).reshape(k, n).astype(np.float32)
    by_word = np.ascontiguousarray(scaled.reshape(k // 512, 128, 4, n).transpose(0, 1, 3, 2))
    if fmt == "e4m3":
        words = by_word.astype(ml_dtypes.float8_e4m3fn).view(np.uint8)
    else:
        c = by_word.astype(ml_dtypes.float4_e2m1fn).view(np.uint8) & 0xF
        words = c[..., 0::2] | (c[..., 1::2] << 4)
    return np.ascontiguousarray(words), np.ascontiguousarray(byte.astype(np.uint8).reshape(k // 512, 16, n))


def unpack_weight(words, scales, fmt):
    g, p, n, _ = words.shape
    if fmt == "e4m3":
        vals = np.ascontiguousarray(words).view(ml_dtypes.float8_e4m3fn).astype(np.float64)
    else:
        nib = np.empty((g, p, n, 4), np.uint8)
        nib[..., 0::2] = words & 0xF
        nib[..., 1::2] = words >> 4
        vals = E2M1[nib]
    vals = vals * np.repeat(np.exp2(scales.astype(np.float64) - 127.0), 8, axis=1)[..., None]
    return vals.transpose(0, 1, 3, 2).reshape(g * 512, n)


N, G, F, K, E = 512, 4096, 128, 4, 1


def setup_inputs():
    s = mx_kscale(N)
    x = bf(np.random.standard_normal((N, G)) * s[:, None])
    stack = np.random.standard_normal((E, N, N)) / np.sqrt(N) / s[:, None] * s[None, :]
    words, scales = pack_weight(stack.reshape(-1, N), "e4m3")
    return {"x": x, "S_words": words, "S_scales": scales}


def reference(x, S_words, S_scales):
    Sq = unpack_weight(S_words, S_scales, "e4m3").reshape(E, N, N)
    z0 = np.broadcast_to(f64(x).T[None], (E, G, N))
    z1 = mxq(z0, 2, "e4m3") @ Sq
    z2 = mxq(z1, 2, "e4m3") @ Sq
    return z1, z2

@@ -1,0 +1,156 @@
+from contextlib import ExitStack
+
+import concourse.mybir as mybir
+from concourse.masks import make_identity
+
+F32 = mybir.dt.float32
+BF16 = mybir.dt.bfloat16
+I32 = mybir.dt.int32
+U32 = mybir.dt.uint32
+U8 = mybir.dt.uint8
+FP8X4 = mybir.dt.float8_e4m3fn_x4
+
+P = 128
+PACK = 4
+NODES = P * PACK
+FEATURES = 4096
+TILES = 4
+CHUNK = TILES * P
+CHUNKS = FEATURES // CHUNK
+QUADRANTS = 4
+
+ACC_BANKS = 5
+TURN_BANKS = 3
+STAGES = 6
+
+FLOPS = 2 * 2 * FEATURES * NODES * NODES
+
+
+def tile_graphfilter_pa_t_e_kernel(tc, x, S_words, S_scales, out_0, out_1):
+    nc = tc.nc
+
+    x_chunks = x.rearrange("(p j) (c f) -> c p j f", j=PACK, f=CHUNK)
+    z1_chunks = out_0[0].rearrange("(c i r) n -> c i r n", i=P, r=TILES)
+    z2_chunks = out_1[0].rearrange("(c i r) n -> c i r n", i=P, r=TILES)
+    s_word_rows = S_words[0].rearrange("p n t -> p (n t)").bitcast(I32)
+    s_scale_rows = S_scales[0].bitcast(I32)
+
+    with ExitStack() as ctx:
+        consts = ctx.enter_context(tc.tile_pool(name="consts", bufs=1))
+        raw_pool = ctx.enter_context(tc.tile_pool(name="raw", bufs=CHUNKS))
+        x_pool = ctx.enter_context(tc.tile_pool(name="xq", bufs=3))
+        z_pool = ctx.enter_context(tc.tile_pool(name="zq", bufs=2))
+        stage_pool = ctx.enter_context(tc.tile_pool(name="stage", bufs=STAGES))
+        acc_pool = ctx.enter_context(tc.psum_pool(name="acc", bufs=ACC_BANKS))
+        turn_pool = ctx.enter_context(tc.psum_pool(name="turn", bufs=TURN_BANKS))
+        ctx.enter_context(tc.manual_schedule())
+
+        s_scales = consts.tile([P, NODES], U8, align_bytes=64)
+        nc.vector.memset(s_scales[:].bitcast(I32), 0)
+        s_codes = consts.tile([P, NODES], U32, align_bytes=64)
+        identity = consts.tile([P, P], F32)
+        make_identity(nc, identity[:])
+
+        x_raw = []
+
+        def load_x(c):
+            raw = raw_pool.tile([P, PACK, CHUNK], BF16)
+            nc.sync.dma_start(out=raw[:], in_=x_chunks[c])
+            x_raw.append(raw)
+
+        load_x(0)
+        for q in range(QUADRANTS):
+            nc.sync.dma_start(
+                out=s_scales[32 * q : 32 * q + PACK, :].bitcast(I32),
+                in_=s_scale_rows[PACK * q : PACK * (q + 1), :],
+            )
+        nc.sync.dma_start(out=s_codes[:].bitcast(I32), in_=s_word_rows)
+        for c in range(1, CHUNKS):
+            load_x(c)
+
+        x_grouped = {}
+        x_codes = {}
+        x_scales = {}
+        z1_stage = {}
+        z1_codes = {}
+        z1_scales = {}
+
+        def regroup_x(c):
+            grouped = x_pool.tile([P, TILES, P, PACK], BF16, align_bytes=64)
+            nc.vector.tensor_copy(
+                out=grouped[:].rearrange("p r i j -> p i j r"),
+                in_=x_raw[c][:].rearrange("p j (i r) -> p i j r", r=TILES),
+            )
+            x_grouped[c] = grouped
+
+        def quantise_x(c):
+            codes = x_pool.tile([P, CHUNK], U32, align_bytes=64)
+            scales = x_pool.tile([P, CHUNK], U8, align_bytes=64)
+            nc.vector.quantize_mx(
+                out=codes[:].bitcast(FP8X4),
+                scales=scales[:],
+                in_=x_grouped[c][:].rearrange("p r i j -> p (r i j)"),
+            )
+            x_codes[c] = codes
+            x_scales[c] = scales
+
+        def product(codes, scales, rows):
+            stage = stage_pool.tile([P, TILES, NODES], F32)
+            for r in range(TILES):
+                cols = slice(r * P, (r + 1) * P)
+                acc = acc_pool.tile([P, NODES], F32)
+                nc.tensor.matmul_mx(
+                    out=acc[:],
+                    lhsT=codes[:, cols].bitcast(FP8X4),
+                    lhsT_scale=scales[:, cols],
+                    rhs=s_codes[:].bitcast(FP8X4),
+                    rhs_scale=s_scales[:],
+                    start=True,
+                    stop=True,
+                )
+                nc.scalar.copy(out=stage[:, r, :], in_=acc[:])
+            nc.sync.dma_start(out=rows, in_=stage[:])
+            return stage
+
+        def turn_and_quantise_z1(c):
+            grouped = z_pool.tile([P, TILES, P, PACK], BF16, align_bytes=64)
+            codes = z_pool.tile([P, CHUNK], U32, align_bytes=64)
+            scales = z_pool.tile([P, CHUNK], U8, align_bytes=64)
+
+            def quantise_tile(r):
+                cols = slice(r * P, (r + 1) * P)
+                nc.vector.quantize_mx(
+                    out=codes[:, cols].bitcast(FP8X4),
+                    scales=scales[:, cols],
+                    in_=grouped[:, r, :, :].rearrange("p i t -> p (i t)"),
+                )
+
+            for r in range(TILES):
+                turned = turn_pool.tile([P, PACK, P], F32)
+                for t in range(PACK):
+                    nc.tensor.transpose(
+                        turned[:, t, :], z1_stage[c][:, r, t:NODES:PACK], identity[:]
+                    )
+                nc.vector.tensor_copy(
+                    out=grouped[:, r, :, :], in_=turned[:].rearrange("p t i -> p i t")
+                )
+                if r > 0:
+                    quantise_tile(r - 1)
+            quantise_tile(TILES - 1)
+            z1_codes[c] = codes
+            z1_scales[c] = scales
+
+        regroup_x(0)
+        quantise_x(0)
+        regroup_x(1)
+        for c in range(CHUNKS + 1):
+            if c < CHUNKS:
+                z1_stage[c] = product(x_codes[c], x_scales[c], z1_chunks[c])
+            if c >= 1:
+                product(z1_codes[c - 1], z1_scales[c - 1], z2_chunks[c - 1])
+            if c + 1 < CHUNKS:
+                quantise_x(c + 1)
+            if c + 2 < CHUNKS:
+                regroup_x(c + 2)
+            if c < CHUNKS:
+                turn_and_quantise_z1(c)

@@ -21,6 +21,7 @@ QUADRANTS = 4
 
 ACC_BANKS = 5
 TURN_BANKS = 3
+VECTOR_CHUNKS = 2
 STAGES = 6
 
 FLOPS = 2 * 2 * FEATURES * NODES * NODES
@@ -72,15 +73,26 @@ def tile_graphfilter_pa_t_e_kernel(tc, x, S_words, S_scales, out_0, out_1):
         x_codes = {}
         x_scales = {}
         z1_stage = {}
+        z1_grouped = {}
         z1_codes = {}
         z1_scales = {}
 
         def regroup_x(c):
             grouped = x_pool.tile([P, TILES, P, PACK], BF16, align_bytes=64)
-            nc.vector.tensor_copy(
-                out=grouped[:].rearrange("p r i j -> p i j r"),
-                in_=x_raw[c][:].rearrange("p j (i r) -> p i j r", r=TILES),
-            )
+            if c < VECTOR_CHUNKS:
+                nc.vector.tensor_copy(
+                    out=grouped[:].rearrange("p r i j -> p i j r"),
+                    in_=x_raw[c][:].rearrange("p j (i r) -> p i j r", r=TILES),
+                )
+            else:
+                nc.gpsimd.tensor_scalar(
+                    out=grouped[:],
+                    in0=x_raw[c][:].rearrange("p j (i r) -> p r i j", r=TILES),
+                    scalar1=1.0,
+                    scalar2=0.0,
+                    op0=mybir.AluOpType.mult,
+                    op1=mybir.AluOpType.add,
+                )
             x_grouped[c] = grouped
 
         def quantise_x(c):
@@ -112,18 +124,21 @@ def tile_graphfilter_pa_t_e_kernel(tc, x, S_words, S_scales, out_0, out_1):
             nc.sync.dma_start(out=rows, in_=stage[:])
             return stage
 
-        def turn_and_quantise_z1(c):
+        def quantise_z1_tile(c, r):
+            cols = slice(r * P, (r + 1) * P)
+            nc.vector.quantize_mx(
+                out=z1_codes[c][:, cols].bitcast(FP8X4),
+                scales=z1_scales[c][:, cols],
+                in_=z1_grouped[c][:, r, :, :].rearrange("p i t -> p (i t)"),
+            )
+
+        def turn_z1(c):
             grouped = z_pool.tile([P, TILES, P, PACK], BF16, align_bytes=64)
             codes = z_pool.tile([P, CHUNK], U32, align_bytes=64)
             scales = z_pool.tile([P, CHUNK], U8, align_bytes=64)
-
-            def quantise_tile(r):
-                cols = slice(r * P, (r + 1) * P)
-                nc.vector.quantize_mx(
-                    out=codes[:, cols].bitcast(FP8X4),
-                    scales=scales[:, cols],
-                    in_=grouped[:, r, :, :].rearrange("p i t -> p (i t)"),
-                )
+            z1_grouped[c] = grouped
+            z1_codes[c] = codes
+            z1_scales[c] = scales
 
             for r in range(TILES):
                 turned = turn_pool.tile([P, PACK, P], F32)
@@ -135,22 +150,23 @@ def tile_graphfilter_pa_t_e_kernel(tc, x, S_words, S_scales, out_0, out_1):
                     out=grouped[:, r, :, :], in_=turned[:].rearrange("p t i -> p i t")
                 )
                 if r > 0:
-                    quantise_tile(r - 1)
-            quantise_tile(TILES - 1)
-            z1_codes[c] = codes
-            z1_scales[c] = scales
+                    quantise_z1_tile(c, r - 1)
 
-        regroup_x(0)
-        quantise_x(0)
-        regroup_x(1)
+        for c in range(2):
+            regroup_x(c)
+            quantise_x(c)
+        for c in range(2, 4):
+            regroup_x(c)
         for c in range(CHUNKS + 1):
             if c < CHUNKS:
                 z1_stage[c] = product(x_codes[c], x_scales[c], z1_chunks[c])
             if c >= 1:
                 product(z1_codes[c - 1], z1_scales[c - 1], z2_chunks[c - 1])
-            if c + 1 < CHUNKS:
-                quantise_x(c + 1)
-            if c + 2 < CHUNKS:
-                regroup_x(c + 2)
             if c < CHUNKS:
-                turn_and_quantise_z1(c)
+                turn_z1(c)
+            if c + 2 < CHUNKS:
+                quantise_x(c + 2)
+            if c < CHUNKS:
+                quantise_z1_tile(c, TILES - 1)
+            if c + 4 < CHUNKS:
+                regroup_x(c + 4)

@@ -14,15 +14,18 @@ P = 128
 PACK = 4
 NODES = P * PACK
 FEATURES = 4096
-TILES = 4
+TILES = 2
 CHUNK = TILES * P
 CHUNKS = FEATURES // CHUNK
+LOAD_CHUNKS = 2
+LOADS = CHUNKS // LOAD_CHUNKS
 QUADRANTS = 4
 
-ACC_BANKS = 5
-TURN_BANKS = 3
-VECTOR_CHUNKS = 2
-STAGES = 6
+ACC_BANKS = 4
+TURN_BANKS = 4
+TURN_LAG = 1
+Z2_LAG = 3
+STAGES = 12
 
 FLOPS = 2 * 2 * FEATURES * NODES * NODES
 
@@ -30,7 +33,7 @@ FLOPS = 2 * 2 * FEATURES * NODES * NODES
 def tile_graphfilter_pa_t_e_kernel(tc, x, S_words, S_scales, out_0, out_1):
     nc = tc.nc
 
-    x_chunks = x.rearrange("(p j) (c f) -> c p j f", j=PACK, f=CHUNK)
+    x_loads = x.rearrange("(p j) (l f) -> l p j f", j=PACK, f=LOAD_CHUNKS * CHUNK)
     z1_chunks = out_0[0].rearrange("(c i r) n -> c i r n", i=P, r=TILES)
     z2_chunks = out_1[0].rearrange("(c i r) n -> c i r n", i=P, r=TILES)
     s_word_rows = S_words[0].rearrange("p n t -> p (n t)").bitcast(I32)
@@ -38,9 +41,9 @@ def tile_graphfilter_pa_t_e_kernel(tc, x, S_words, S_scales, out_0, out_1):
 
     with ExitStack() as ctx:
         consts = ctx.enter_context(tc.tile_pool(name="consts", bufs=1))
-        raw_pool = ctx.enter_context(tc.tile_pool(name="raw", bufs=CHUNKS))
+        raw_pool = ctx.enter_context(tc.tile_pool(name="raw", bufs=LOADS))
         x_pool = ctx.enter_context(tc.tile_pool(name="xq", bufs=3))
-        z_pool = ctx.enter_context(tc.tile_pool(name="zq", bufs=2))
+        z_pool = ctx.enter_context(tc.tile_pool(name="zq", bufs=Z2_LAG))
         stage_pool = ctx.enter_context(tc.tile_pool(name="stage", bufs=STAGES))
         acc_pool = ctx.enter_context(tc.psum_pool(name="acc", bufs=ACC_BANKS))
         turn_pool = ctx.enter_context(tc.psum_pool(name="turn", bufs=TURN_BANKS))
@@ -54,9 +57,9 @@ def tile_graphfilter_pa_t_e_kernel(tc, x, S_words, S_scales, out_0, out_1):
 
         x_raw = []
 
-        def load_x(c):
-            raw = raw_pool.tile([P, PACK, CHUNK], BF16)
-            nc.sync.dma_start(out=raw[:], in_=x_chunks[c])
+        def load_x(l):
+            raw = raw_pool.tile([P, PACK, LOAD_CHUNKS, CHUNK], BF16)
+            nc.sync.dma_start(out=raw[:].rearrange("p j c f -> p j (c f)"), in_=x_loads[l])
             x_raw.append(raw)
 
         load_x(0)
@@ -66,8 +69,8 @@ def tile_graphfilter_pa_t_e_kernel(tc, x, S_words, S_scales, out_0, out_1):
                 in_=s_scale_rows[PACK * q : PACK * (q + 1), :],
             )
         nc.sync.dma_start(out=s_codes[:].bitcast(I32), in_=s_word_rows)
-        for c in range(1, CHUNKS):
-            load_x(c)
+        for l in range(1, LOADS):
+            load_x(l)
 
         x_grouped = {}
         x_codes = {}
@@ -79,20 +82,11 @@ def tile_graphfilter_pa_t_e_kernel(tc, x, S_words, S_scales, out_0, out_1):
 
         def regroup_x(c):
             grouped = x_pool.tile([P, TILES, P, PACK], BF16, align_bytes=64)
-            if c < VECTOR_CHUNKS:
-                nc.vector.tensor_copy(
-                    out=grouped[:].rearrange("p r i j -> p i j r"),
-                    in_=x_raw[c][:].rearrange("p j (i r) -> p i j r", r=TILES),
-                )
-            else:
-                nc.gpsimd.tensor_scalar(
-                    out=grouped[:],
-                    in0=x_raw[c][:].rearrange("p j (i r) -> p r i j", r=TILES),
-                    scalar1=1.0,
-                    scalar2=0.0,
-                    op0=mybir.AluOpType.mult,
-                    op1=mybir.AluOpType.add,
-                )
+            raw = x_raw[c // LOAD_CHUNKS][:, :, c % LOAD_CHUNKS, :]
+            nc.vector.tensor_copy(
+                out=grouped[:].rearrange("p r i j -> p i j r"),
+                in_=raw.rearrange("p j (i r) -> p i j r", r=TILES),
+            )
             x_grouped[c] = grouped
 
         def quantise_x(c):
@@ -155,18 +149,17 @@ def tile_graphfilter_pa_t_e_kernel(tc, x, S_words, S_scales, out_0, out_1):
         for c in range(2):
             regroup_x(c)
             quantise_x(c)
-        for c in range(2, 4):
-            regroup_x(c)
-        for c in range(CHUNKS + 1):
+        regroup_x(2)
+        for c in range(CHUNKS + Z2_LAG):
             if c < CHUNKS:
                 z1_stage[c] = product(x_codes[c], x_scales[c], z1_chunks[c])
-            if c >= 1:
-                product(z1_codes[c - 1], z1_scales[c - 1], z2_chunks[c - 1])
-            if c < CHUNKS:
-                turn_z1(c)
+            if c >= Z2_LAG:
+                product(z1_codes[c - Z2_LAG], z1_scales[c - Z2_LAG], z2_chunks[c - Z2_LAG])
+            if TURN_LAG <= c < CHUNKS + TURN_LAG:
+                turn_z1(c - TURN_LAG)
             if c + 2 < CHUNKS:
                 quantise_x(c + 2)
-            if c < CHUNKS:
-                quantise_z1_tile(c, TILES - 1)
-            if c + 4 < CHUNKS:
-                regroup_x(c + 4)
+            if TURN_LAG <= c < CHUNKS + TURN_LAG:
+                quantise_z1_tile(c - TURN_LAG, TILES - 1)
+            if c + 3 < CHUNKS:
+                regroup_x(c + 3)

@@ -1,7 +1,6 @@
 from contextlib import ExitStack
 
 import concourse.mybir as mybir
-from concourse.masks import make_identity
 
 F32 = mybir.dt.float32
 BF16 = mybir.dt.bfloat16
@@ -23,8 +22,7 @@ QUADRANTS = 4
 
 ACC_BANKS = 4
 TURN_BANKS = 4
-TURN_LAG = 1
-Z2_LAG = 3
+Z2_LAG = 2
 STAGES = 12
 
 FLOPS = 2 * 2 * FEATURES * NODES * NODES
@@ -43,7 +41,7 @@ def tile_graphfilter_pa_t_e_kernel(tc, x, S_words, S_scales, out_0, out_1):
         consts = ctx.enter_context(tc.tile_pool(name="consts", bufs=1))
         raw_pool = ctx.enter_context(tc.tile_pool(name="raw", bufs=LOADS))
         x_pool = ctx.enter_context(tc.tile_pool(name="xq", bufs=3))
-        z_pool = ctx.enter_context(tc.tile_pool(name="zq", bufs=Z2_LAG))
+        z_pool = ctx.enter_context(tc.tile_pool(name="zq", bufs=Z2_LAG + 1))
         stage_pool = ctx.enter_context(tc.tile_pool(name="stage", bufs=STAGES))
         acc_pool = ctx.enter_context(tc.psum_pool(name="acc", bufs=ACC_BANKS))
         turn_pool = ctx.enter_context(tc.psum_pool(name="turn", bufs=TURN_BANKS))
@@ -52,8 +50,8 @@ def tile_graphfilter_pa_t_e_kernel(tc, x, S_words, S_scales, out_0, out_1):
         s_scales = consts.tile([P, NODES], U8, align_bytes=64)
         nc.vector.memset(s_scales[:].bitcast(I32), 0)
         s_codes = consts.tile([P, NODES], U32, align_bytes=64)
-        identity = consts.tile([P, P], F32)
-        make_identity(nc, identity[:])
+        s_sorted_codes = consts.tile([P, NODES], U32, align_bytes=64)
+        s_sorted_scales = consts.tile([P, NODES], U8, align_bytes=64)
 
         x_raw = []
 
@@ -75,7 +73,6 @@ def tile_graphfilter_pa_t_e_kernel(tc, x, S_words, S_scales, out_0, out_1):
         x_grouped = {}
         x_codes = {}
         x_scales = {}
-        z1_stage = {}
         z1_grouped = {}
         z1_codes = {}
         z1_scales = {}
@@ -116,7 +113,6 @@ def tile_graphfilter_pa_t_e_kernel(tc, x, S_words, S_scales, out_0, out_1):
                 )
                 nc.scalar.copy(out=stage[:, r, :], in_=acc[:])
             nc.sync.dma_start(out=rows, in_=stage[:])
-            return stage
 
         def quantise_z1_tile(c, r):
             cols = slice(r * P, (r + 1) * P)
@@ -124,6 +120,16 @@ def tile_graphfilter_pa_t_e_kernel(tc, x, S_words, S_scales, out_0, out_1):
                 out=z1_codes[c][:, cols].bitcast(FP8X4),
                 scales=z1_scales[c][:, cols],
                 in_=z1_grouped[c][:, r, :, :].rearrange("p i t -> p (i t)"),
+            )
+
+        def sort_s():
+            nc.vector.tensor_copy(
+                out=s_sorted_codes[:].bitcast(I32).rearrange("p (t m) -> p t m", t=PACK),
+                in_=s_codes[:].bitcast(I32).rearrange("p (m t) -> p t m", t=PACK),
+            )
+            nc.vector.tensor_copy(
+                out=s_sorted_scales[:].rearrange("p (t m) -> p m t", t=PACK),
+                in_=s_scales[:].rearrange("p (m t) -> p m t", t=PACK),
             )
 
         def turn_z1(c):
@@ -135,10 +141,18 @@ def tile_graphfilter_pa_t_e_kernel(tc, x, S_words, S_scales, out_0, out_1):
             z1_scales[c] = scales
 
             for r in range(TILES):
+                cols = slice(r * P, (r + 1) * P)
                 turned = turn_pool.tile([P, PACK, P], F32)
                 for t in range(PACK):
-                    nc.tensor.transpose(
-                        turned[:, t, :], z1_stage[c][:, r, t:NODES:PACK], identity[:]
+                    nodes = slice(t * P, (t + 1) * P)
+                    nc.tensor.matmul_mx(
+                        out=turned[:, t, :],
+                        lhsT=s_sorted_codes[:, nodes].bitcast(FP8X4),
+                        lhsT_scale=s_sorted_scales[:, nodes],
+                        rhs=x_codes[c][:, cols].bitcast(FP8X4),
+                        rhs_scale=x_scales[c][:, cols],
+                        start=True,
+                        stop=True,
                     )
                 nc.vector.tensor_copy(
                     out=grouped[:, r, :, :], in_=turned[:].rearrange("p t i -> p i t")
@@ -146,20 +160,22 @@ def tile_graphfilter_pa_t_e_kernel(tc, x, S_words, S_scales, out_0, out_1):
                 if r > 0:
                     quantise_z1_tile(c, r - 1)
 
-        for c in range(2):
-            regroup_x(c)
-            quantise_x(c)
+        regroup_x(0)
+        quantise_x(0)
+        sort_s()
+        regroup_x(1)
+        quantise_x(1)
         regroup_x(2)
         for c in range(CHUNKS + Z2_LAG):
             if c < CHUNKS:
-                z1_stage[c] = product(x_codes[c], x_scales[c], z1_chunks[c])
+                product(x_codes[c], x_scales[c], z1_chunks[c])
             if c >= Z2_LAG:
                 product(z1_codes[c - Z2_LAG], z1_scales[c - Z2_LAG], z2_chunks[c - Z2_LAG])
-            if TURN_LAG <= c < CHUNKS + TURN_LAG:
-                turn_z1(c - TURN_LAG)
+            if c < CHUNKS:
+                turn_z1(c)
             if c + 2 < CHUNKS:
                 quantise_x(c + 2)
-            if TURN_LAG <= c < CHUNKS + TURN_LAG:
-                quantise_z1_tile(c - TURN_LAG, TILES - 1)
+            if c < CHUNKS:
+                quantise_z1_tile(c, TILES - 1)
             if c + 3 < CHUNKS:
                 regroup_x(c + 3)

@@ -16,13 +16,13 @@ FEATURES = 4096
 TILES = 2
 CHUNK = TILES * P
 CHUNKS = FEATURES // CHUNK
-LOAD_CHUNKS = 2
-LOADS = CHUNKS // LOAD_CHUNKS
+LOAD_CHUNKS = (1, 1, 2, 4, 8)
 QUADRANTS = 4
 
 ACC_BANKS = 4
 TURN_BANKS = 4
-Z2_LAG = 2
+Z2_LAG = 1
+SCALAR_TURNS = 4
 STAGES = 12
 
 FLOPS = 2 * 2 * FEATURES * NODES * NODES
@@ -31,7 +31,7 @@ FLOPS = 2 * 2 * FEATURES * NODES * NODES
 def tile_graphfilter_pa_t_e_kernel(tc, x, S_words, S_scales, out_0, out_1):
     nc = tc.nc
 
-    x_loads = x.rearrange("(p j) (l f) -> l p j f", j=PACK, f=LOAD_CHUNKS * CHUNK)
+    x_rows = x.rearrange("(p j) f -> p j f", j=PACK)
     z1_chunks = out_0[0].rearrange("(c i r) n -> c i r n", i=P, r=TILES)
     z2_chunks = out_1[0].rearrange("(c i r) n -> c i r n", i=P, r=TILES)
     s_word_rows = S_words[0].rearrange("p n t -> p (n t)").bitcast(I32)
@@ -39,9 +39,9 @@ def tile_graphfilter_pa_t_e_kernel(tc, x, S_words, S_scales, out_0, out_1):
 
     with ExitStack() as ctx:
         consts = ctx.enter_context(tc.tile_pool(name="consts", bufs=1))
-        raw_pool = ctx.enter_context(tc.tile_pool(name="raw", bufs=LOADS))
+        raw_pool = ctx.enter_context(tc.tile_pool(name="raw", bufs=1))
         x_pool = ctx.enter_context(tc.tile_pool(name="xq", bufs=3))
-        z_pool = ctx.enter_context(tc.tile_pool(name="zq", bufs=Z2_LAG + 1))
+        z_pool = ctx.enter_context(tc.tile_pool(name="zq", bufs=3))
         stage_pool = ctx.enter_context(tc.tile_pool(name="stage", bufs=STAGES))
         acc_pool = ctx.enter_context(tc.psum_pool(name="acc", bufs=ACC_BANKS))
         turn_pool = ctx.enter_context(tc.psum_pool(name="turn", bufs=TURN_BANKS))
@@ -55,20 +55,22 @@ def tile_graphfilter_pa_t_e_kernel(tc, x, S_words, S_scales, out_0, out_1):
 
         x_raw = []
 
-        def load_x(l):
-            raw = raw_pool.tile([P, PACK, LOAD_CHUNKS, CHUNK], BF16)
-            nc.sync.dma_start(out=raw[:].rearrange("p j c f -> p j (c f)"), in_=x_loads[l])
-            x_raw.append(raw)
+        def load_x(chunks):
+            first = len(x_raw)
+            raw = raw_pool.tile([P, PACK, chunks * CHUNK], BF16, name="raw%d" % first)
+            nc.sync.dma_start(out=raw[:], in_=x_rows[:, :, first * CHUNK : (first + chunks) * CHUNK])
+            for k in range(chunks):
+                x_raw.append((raw, k * CHUNK))
 
-        load_x(0)
+        load_x(LOAD_CHUNKS[0])
         for q in range(QUADRANTS):
             nc.sync.dma_start(
                 out=s_scales[32 * q : 32 * q + PACK, :].bitcast(I32),
                 in_=s_scale_rows[PACK * q : PACK * (q + 1), :],
             )
         nc.sync.dma_start(out=s_codes[:].bitcast(I32), in_=s_word_rows)
-        for l in range(1, LOADS):
-            load_x(l)
+        for chunks in LOAD_CHUNKS[1:]:
+            load_x(chunks)
 
         x_grouped = {}
         x_codes = {}
@@ -79,10 +81,10 @@ def tile_graphfilter_pa_t_e_kernel(tc, x, S_words, S_scales, out_0, out_1):
 
         def regroup_x(c):
             grouped = x_pool.tile([P, TILES, P, PACK], BF16, align_bytes=64)
-            raw = x_raw[c // LOAD_CHUNKS][:, :, c % LOAD_CHUNKS, :]
+            raw, first = x_raw[c]
             nc.vector.tensor_copy(
                 out=grouped[:].rearrange("p r i j -> p i j r"),
-                in_=raw.rearrange("p j (i r) -> p i j r", r=TILES),
+                in_=raw[:, :, first : first + CHUNK].rearrange("p j (i r) -> p i j r", r=TILES),
             )
             x_grouped[c] = grouped
 
@@ -97,7 +99,7 @@ def tile_graphfilter_pa_t_e_kernel(tc, x, S_words, S_scales, out_0, out_1):
             x_codes[c] = codes
             x_scales[c] = scales
 
-        def product(codes, scales, rows):
+        def product(codes, scales, rows, vector_helps, by_tile):
             stage = stage_pool.tile([P, TILES, NODES], F32)
             for r in range(TILES):
                 cols = slice(r * P, (r + 1) * P)
@@ -111,15 +113,21 @@ def tile_graphfilter_pa_t_e_kernel(tc, x, S_words, S_scales, out_0, out_1):
                     start=True,
                     stop=True,
                 )
-                nc.scalar.copy(out=stage[:, r, :], in_=acc[:])
-            nc.sync.dma_start(out=rows, in_=stage[:])
+                if vector_helps and r == TILES - 1:
+                    nc.vector.tensor_copy(out=stage[:, r, :], in_=acc[:])
+                else:
+                    nc.scalar.copy(out=stage[:, r, :], in_=acc[:])
+                if by_tile:
+                    nc.sync.dma_start(out=rows[:, r, :], in_=stage[:, r, :])
+            if not by_tile:
+                nc.sync.dma_start(out=rows, in_=stage[:])
 
-        def quantise_z1_tile(c, r):
-            cols = slice(r * P, (r + 1) * P)
+        def quantise_z1(c, first, tiles):
+            cols = slice(first * P, (first + tiles) * P)
             nc.vector.quantize_mx(
                 out=z1_codes[c][:, cols].bitcast(FP8X4),
                 scales=z1_scales[c][:, cols],
-                in_=z1_grouped[c][:, r, :, :].rearrange("p i t -> p (i t)"),
+                in_=z1_grouped[c][:, first : first + tiles, :, :].rearrange("p r i t -> p (r i t)"),
             )
 
         def sort_s():
@@ -154,11 +162,10 @@ def tile_graphfilter_pa_t_e_kernel(tc, x, S_words, S_scales, out_0, out_1):
                         start=True,
                         stop=True,
                     )
-                nc.vector.tensor_copy(
-                    out=grouped[:, r, :, :], in_=turned[:].rearrange("p t i -> p i t")
-                )
-                if r > 0:
-                    quantise_z1_tile(c, r - 1)
+                if r == TILES - 1 and c % SCALAR_TURNS == SCALAR_TURNS - 1:
+                    nc.scalar.copy(out=grouped[:, r, :, :], in_=turned[:].rearrange("p t i -> p i t"))
+                else:
+                    nc.vector.tensor_copy(out=grouped[:, r, :, :], in_=turned[:].rearrange("p t i -> p i t"))
 
         regroup_x(0)
         quantise_x(0)
@@ -167,15 +174,20 @@ def tile_graphfilter_pa_t_e_kernel(tc, x, S_words, S_scales, out_0, out_1):
         quantise_x(1)
         regroup_x(2)
         for c in range(CHUNKS + Z2_LAG):
-            if c < CHUNKS:
-                product(x_codes[c], x_scales[c], z1_chunks[c])
-            if c >= Z2_LAG:
-                product(z1_codes[c - Z2_LAG], z1_scales[c - Z2_LAG], z2_chunks[c - Z2_LAG])
+            if c == 0:
+                product(x_codes[c], x_scales[c], z1_chunks[c], False, False)
             if c < CHUNKS:
                 turn_z1(c)
+            if 0 < c < CHUNKS:
+                product(x_codes[c], x_scales[c], z1_chunks[c], False, False)
+            if c >= Z2_LAG:
+                d = c - Z2_LAG
+                product(z1_codes[d], z1_scales[d], z2_chunks[d], c >= CHUNKS - 1, d == CHUNKS - 1)
             if c + 2 < CHUNKS:
                 quantise_x(c + 2)
-            if c < CHUNKS:
-                quantise_z1_tile(c, TILES - 1)
+                quantise_z1(c, 0, TILES)
+            elif c < CHUNKS:
+                for r in range(TILES):
+                    quantise_z1(c, r, 1)
             if c + 3 < CHUNKS:
                 regroup_x(c + 3)

@@ -22,7 +22,7 @@ QUADRANTS = 4
 ACC_BANKS = 4
 TURN_BANKS = 4
 Z2_LAG = 1
-SCALAR_TURNS = 4
+HEAD_CHUNKS = 2
 STAGES = 12
 
 FLOPS = 2 * 2 * FEATURES * NODES * NODES
@@ -162,7 +162,7 @@ def tile_graphfilter_pa_t_e_kernel(tc, x, S_words, S_scales, out_0, out_1):
                         start=True,
                         stop=True,
                     )
-                if r == TILES - 1 and c % SCALAR_TURNS == SCALAR_TURNS - 1:
+                if r == TILES - 1 and c < HEAD_CHUNKS:
                     nc.scalar.copy(out=grouped[:, r, :, :], in_=turned[:].rearrange("p t i -> p i t"))
                 else:
                     nc.vector.tensor_copy(out=grouped[:, r, :, :], in_=turned[:].rearrange("p t i -> p i t"))

@@ -16,14 +16,15 @@ FEATURES = 4096
 TILES = 2
 CHUNK = TILES * P
 CHUNKS = FEATURES // CHUNK
-LOAD_CHUNKS = (1, 1, 2, 4, 8)
+BLOCK_CHUNKS = (1, 1, 2, 2, 2, 2, 2, 2, 1, 1)
+LOAD_BLOCKS = (1, 1, 1, 2, 5)
 QUADRANTS = 4
 
 ACC_BANKS = 4
 TURN_BANKS = 4
 Z2_LAG = 1
 HEAD_CHUNKS = 2
-STAGES = 12
+STAGES = 8
 
 FLOPS = 2 * 2 * FEATURES * NODES * NODES
 
@@ -32,8 +33,6 @@ def tile_graphfilter_pa_t_e_kernel(tc, x, S_words, S_scales, out_0, out_1):
     nc = tc.nc
 
     x_rows = x.rearrange("(p j) f -> p j f", j=PACK)
-    z1_chunks = out_0[0].rearrange("(c i r) n -> c i r n", i=P, r=TILES)
-    z2_chunks = out_1[0].rearrange("(c i r) n -> c i r n", i=P, r=TILES)
     s_word_rows = S_words[0].rearrange("p n t -> p (n t)").bitcast(I32)
     s_scale_rows = S_scales[0].bitcast(I32)
 
@@ -53,38 +52,50 @@ def tile_graphfilter_pa_t_e_kernel(tc, x, S_words, S_scales, out_0, out_1):
         s_sorted_codes = consts.tile([P, NODES], U32, align_bytes=64)
         s_sorted_scales = consts.tile([P, NODES], U8, align_bytes=64)
 
+        block_of = []
+        for chunks in BLOCK_CHUNKS:
+            first = len(block_of)
+            block_of.extend([(first, chunks)] * chunks)
+
         x_raw = []
 
-        def load_x(chunks):
+        def load_x(blocks):
             first = len(x_raw)
+            chunks = 0
+            for k in range(blocks):
+                chunks += block_of[first + chunks][1]
             raw = raw_pool.tile([P, PACK, chunks * CHUNK], BF16, name="raw%d" % first)
             nc.sync.dma_start(out=raw[:], in_=x_rows[:, :, first * CHUNK : (first + chunks) * CHUNK])
-            for k in range(chunks):
-                x_raw.append((raw, k * CHUNK))
+            x_raw.extend([(raw, first)] * chunks)
 
-        load_x(LOAD_CHUNKS[0])
+        load_x(LOAD_BLOCKS[0])
         for q in range(QUADRANTS):
             nc.sync.dma_start(
                 out=s_scales[32 * q : 32 * q + PACK, :].bitcast(I32),
                 in_=s_scale_rows[PACK * q : PACK * (q + 1), :],
             )
         nc.sync.dma_start(out=s_codes[:].bitcast(I32), in_=s_word_rows)
-        for chunks in LOAD_CHUNKS[1:]:
-            load_x(chunks)
+        for blocks in LOAD_BLOCKS[1:]:
+            load_x(blocks)
 
         x_grouped = {}
         x_codes = {}
         x_scales = {}
+        z1_stages = {}
+        z2_stages = {}
         z1_grouped = {}
         z1_codes = {}
         z1_scales = {}
 
         def regroup_x(c):
             grouped = x_pool.tile([P, TILES, P, PACK], BF16, align_bytes=64)
-            raw, first = x_raw[c]
+            raw, raw_first = x_raw[c]
+            first, chunks = block_of[c]
+            block = raw[:, :, (first - raw_first) * CHUNK : (first - raw_first + chunks) * CHUNK]
+            tiles = slice((c - first) * TILES, (c - first + 1) * TILES)
             nc.vector.tensor_copy(
                 out=grouped[:].rearrange("p r i j -> p i j r"),
-                in_=raw[:, :, first : first + CHUNK].rearrange("p j (i r) -> p i j r", r=TILES),
+                in_=block.rearrange("p j (i r) -> p i j r", r=chunks * TILES)[:, :, :, tiles],
             )
             x_grouped[c] = grouped
 
@@ -99,10 +110,15 @@ def tile_graphfilter_pa_t_e_kernel(tc, x, S_words, S_scales, out_0, out_1):
             x_codes[c] = codes
             x_scales[c] = scales
 
-        def product(codes, scales, rows, vector_helps, by_tile):
-            stage = stage_pool.tile([P, TILES, NODES], F32)
-            for r in range(TILES):
-                cols = slice(r * P, (r + 1) * P)
+        def product(c, codes, scales, out, stages, vector_helps, by_tile):
+            first, chunks = block_of[c]
+            rows = out[0][first * CHUNK : (first + chunks) * CHUNK, :].rearrange("(i r) n -> i r n", i=P)
+            if c == first:
+                stage = stage_pool.tile([P, max(BLOCK_CHUNKS) * TILES, NODES], F32)
+                stages[first] = stage
+            stage = stages[first]
+            for r in range((c - first) * TILES, (c - first + 1) * TILES):
+                cols = slice(r % TILES * P, (r % TILES + 1) * P)
                 acc = acc_pool.tile([P, NODES], F32)
                 nc.tensor.matmul_mx(
                     out=acc[:],
@@ -113,14 +129,14 @@ def tile_graphfilter_pa_t_e_kernel(tc, x, S_words, S_scales, out_0, out_1):
                     start=True,
                     stop=True,
                 )
-                if vector_helps and r == TILES - 1:
+                if vector_helps and r % TILES == TILES - 1:
                     nc.vector.tensor_copy(out=stage[:, r, :], in_=acc[:])
                 else:
                     nc.scalar.copy(out=stage[:, r, :], in_=acc[:])
                 if by_tile:
                     nc.sync.dma_start(out=rows[:, r, :], in_=stage[:, r, :])
-            if not by_tile:
-                nc.sync.dma_start(out=rows, in_=stage[:])
+            if not by_tile and c == first + chunks - 1:
+                nc.sync.dma_start(out=rows, in_=stage[:, : chunks * TILES, :])
 
         def quantise_z1(c, first, tiles):
             cols = slice(first * P, (first + tiles) * P)
@@ -175,14 +191,14 @@ def tile_graphfilter_pa_t_e_kernel(tc, x, S_words, S_scales, out_0, out_1):
         regroup_x(2)
         for c in range(CHUNKS + Z2_LAG):
             if c == 0:
-                product(x_codes[c], x_scales[c], z1_chunks[c], False, False)
+                product(c, x_codes[c], x_scales[c], out_0, z1_stages, False, False)
             if c < CHUNKS:
                 turn_z1(c)
             if 0 < c < CHUNKS:
-                product(x_codes[c], x_scales[c], z1_chunks[c], False, False)
+                product(c, x_codes[c], x_scales[c], out_0, z1_stages, False, False)
             if c >= Z2_LAG:
                 d = c - Z2_LAG
-                product(z1_codes[d], z1_scales[d], z2_chunks[d], c >= CHUNKS - 1, d == CHUNKS - 1)
+                product(d, z1_codes[d], z1_scales[d], out_1, z2_stages, c >= CHUNKS - 1, d == CHUNKS - 1)
             if c + 2 < CHUNKS:
                 quantise_x(c + 2)
                 quantise_z1(c, 0, TILES)

@@ -64,7 +64,7 @@ def tile_graphfilter_pa_t_e_kernel(tc, x, S_words, S_scales, out_0, out_1):
             chunks = 0
             for k in range(blocks):
                 chunks += block_of[first + chunks][1]
-            raw = raw_pool.tile([P, PACK, chunks * CHUNK], BF16, name="raw%d" % first)
+            raw = raw_pool.tile([P, PACK, chunks * CHUNK], BF16, name="raw%d" % first, align_bytes=256)
             nc.sync.dma_start(out=raw[:], in_=x_rows[:, :, first * CHUNK : (first + chunks) * CHUNK])
             x_raw.extend([(raw, first)] * chunks)
 
@@ -114,7 +114,7 @@ def tile_graphfilter_pa_t_e_kernel(tc, x, S_words, S_scales, out_0, out_1):
             first, chunks = block_of[c]
             rows = out[0][first * CHUNK : (first + chunks) * CHUNK, :].rearrange("(i r) n -> i r n", i=P)
             if c == first:
-                stage = stage_pool.tile([P, max(BLOCK_CHUNKS) * TILES, NODES], F32)
+                stage = stage_pool.tile([P, max(BLOCK_CHUNKS) * TILES, NODES], F32, align_bytes=256)
                 stages[first] = stage
             stage = stages[first]
             for r in range((c - first) * TILES, (c - first + 1) * TILES):

from contextlib import ExitStack

import concourse.mybir as mybir

F32 = mybir.dt.float32
BF16 = mybir.dt.bfloat16
I32 = mybir.dt.int32
U32 = mybir.dt.uint32
U8 = mybir.dt.uint8
FP8X4 = mybir.dt.float8_e4m3fn_x4

P = 128
PACK = 4
NODES = P * PACK
FEATURES = 4096
TILES = 2
CHUNK = TILES * P
CHUNKS = FEATURES // CHUNK
BLOCK_CHUNKS = (1, 1, 2, 2, 2, 2, 2, 2, 1, 1)
LOAD_BLOCKS = (1, 1, 1, 2, 5)
QUADRANTS = 4

ACC_BANKS = 4
TURN_BANKS = 4
Z2_LAG = 1
HEAD_CHUNKS = 2
STAGES = 8

FLOPS = 2 * 2 * FEATURES * NODES * NODES


def tile_graphfilter_pa_t_e_kernel(tc, x, S_words, S_scales, out_0, out_1):
    nc = tc.nc

    x_rows = x.rearrange("(p j) f -> p j f", j=PACK)
    s_word_rows = S_words[0].rearrange("p n t -> p (n t)").bitcast(I32)
    s_scale_rows = S_scales[0].bitcast(I32)

    with ExitStack() as ctx:
        consts = ctx.enter_context(tc.tile_pool(name="consts", bufs=1))
        raw_pool = ctx.enter_context(tc.tile_pool(name="raw", bufs=1))
        x_pool = ctx.enter_context(tc.tile_pool(name="xq", bufs=3))
        z_pool = ctx.enter_context(tc.tile_pool(name="zq", bufs=3))
        stage_pool = ctx.enter_context(tc.tile_pool(name="stage", bufs=STAGES))
        acc_pool = ctx.enter_context(tc.psum_pool(name="acc", bufs=ACC_BANKS))
        turn_pool = ctx.enter_context(tc.psum_pool(name="turn", bufs=TURN_BANKS))
        ctx.enter_context(tc.manual_schedule())

        s_scales = consts.tile([P, NODES], U8, align_bytes=64)
        nc.vector.memset(s_scales[:].bitcast(I32), 0)
        s_codes = consts.tile([P, NODES], U32, align_bytes=64)
        s_sorted_codes = consts.tile([P, NODES], U32, align_bytes=64)
        s_sorted_scales = consts.tile([P, NODES], U8, align_bytes=64)

        block_of = []
        for chunks in BLOCK_CHUNKS:
            first = len(block_of)
            block_of.extend([(first, chunks)] * chunks)

        x_raw = []

        def load_x(blocks):
            first = len(x_raw)
            chunks = 0
            for k in range(blocks):
                chunks += block_of[first + chunks][1]
            raw = raw_pool.tile([P, PACK, chunks * CHUNK], BF16, name="raw%d" % first, align_bytes=256)
            nc.sync.dma_start(out=raw[:], in_=x_rows[:, :, first * CHUNK : (first + chunks) * CHUNK])
            x_raw.extend([(raw, first)] * chunks)

        load_x(LOAD_BLOCKS[0])
        for q in range(QUADRANTS):
            nc.sync.dma_start(
                out=s_scales[32 * q : 32 * q + PACK, :].bitcast(I32),
                in_=s_scale_rows[PACK * q : PACK * (q + 1), :],
            )
        nc.sync.dma_start(out=s_codes[:].bitcast(I32), in_=s_word_rows)
        for blocks in LOAD_BLOCKS[1:]:
            load_x(blocks)

        x_grouped = {}
        x_codes = {}
        x_scales = {}
        z1_stages = {}
        z2_stages = {}
        z1_grouped = {}
        z1_codes = {}
        z1_scales = {}

        def regroup_x(c):
            grouped = x_pool.tile([P, TILES, P, PACK], BF16, align_bytes=64)
            raw, raw_first = x_raw[c]
            first, chunks = block_of[c]
            block = raw[:, :, (first - raw_first) * CHUNK : (first - raw_first + chunks) * CHUNK]
            tiles = slice((c - first) * TILES, (c - first + 1) * TILES)
            nc.vector.tensor_copy(
                out=grouped[:].rearrange("p r i j -> p i j r"),
                in_=block.rearrange("p j (i r) -> p i j r", r=chunks * TILES)[:, :, :, tiles],
            )
            x_grouped[c] = grouped

        def quantise_x(c):
            codes = x_pool.tile([P, CHUNK], U32, align_bytes=64)
            scales = x_pool.tile([P, CHUNK], U8, align_bytes=64)
            nc.vector.quantize_mx(
                out=codes[:].bitcast(FP8X4),
                scales=scales[:],
                in_=x_grouped[c][:].rearrange("p r i j -> p (r i j)"),
            )
            x_codes[c] = codes
            x_scales[c] = scales

        def product(c, codes, scales, out, stages, vector_helps, by_tile):
            first, chunks = block_of[c]
            rows = out[0][first * CHUNK : (first + chunks) * CHUNK, :].rearrange("(i r) n -> i r n", i=P)
            if c == first:
                stage = stage_pool.tile([P, max(BLOCK_CHUNKS) * TILES, NODES], F32, align_bytes=256)
                stages[first] = stage
            stage = stages[first]
            for r in range((c - first) * TILES, (c - first + 1) * TILES):
                cols = slice(r % TILES * P, (r % TILES + 1) * P)
                acc = acc_pool.tile([P, NODES], F32)
                nc.tensor.matmul_mx(
                    out=acc[:],
                    lhsT=codes[:, cols].bitcast(FP8X4),
                    lhsT_scale=scales[:, cols],
                    rhs=s_codes[:].bitcast(FP8X4),
                    rhs_scale=s_scales[:],
                    start=True,
                    stop=True,
                )
                if vector_helps and r % TILES == TILES - 1:
                    nc.vector.tensor_copy(out=stage[:, r, :], in_=acc[:])
                else:
                    nc.scalar.copy(out=stage[:, r, :], in_=acc[:])
                if by_tile:
                    nc.sync.dma_start(out=rows[:, r, :], in_=stage[:, r, :])
            if not by_tile and c == first + chunks - 1:
                nc.sync.dma_start(out=rows, in_=stage[:, : chunks * TILES, :])

        def quantise_z1(c, first, tiles):
            cols = slice(first * P, (first + tiles) * P)
            nc.vector.quantize_mx(
                out=z1_codes[c][:, cols].bitcast(FP8X4),
                scales=z1_scales[c][:, cols],
                in_=z1_grouped[c][:, first : first + tiles, :, :].rearrange("p r i t -> p (r i t)"),
            )

        def sort_s():
            nc.vector.tensor_copy(
                out=s_sorted_codes[:].bitcast(I32).rearrange("p (t m) -> p t m", t=PACK),
                in_=s_codes[:].bitcast(I32).rearrange("p (m t) -> p t m", t=PACK),
            )
            nc.vector.tensor_copy(
                out=s_sorted_scales[:].rearrange("p (t m) -> p m t", t=PACK),
                in_=s_scales[:].rearrange("p (m t) -> p m t", t=PACK),
            )

        def turn_z1(c):
            grouped = z_pool.tile([P, TILES, P, PACK], BF16, align_bytes=64)
            codes = z_pool.tile([P, CHUNK], U32, align_bytes=64)
            scales = z_pool.tile([P, CHUNK], U8, align_bytes=64)
            z1_grouped[c] = grouped
            z1_codes[c] = codes
            z1_scales[c] = scales

            for r in range(TILES):
                cols = slice(r * P, (r + 1) * P)
                turned = turn_pool.tile([P, PACK, P], F32)
                for t in range(PACK):
                    nodes = slice(t * P, (t + 1) * P)
                    nc.tensor.matmul_mx(
                        out=turned[:, t, :],
                        lhsT=s_sorted_codes[:, nodes].bitcast(FP8X4),
                        lhsT_scale=s_sorted_scales[:, nodes],
                        rhs=x_codes[c][:, cols].bitcast(FP8X4),
                        rhs_scale=x_scales[c][:, cols],
                        start=True,
                        stop=True,
                    )
                if r == TILES - 1 and c < HEAD_CHUNKS:
                    nc.scalar.copy(out=grouped[:, r, :, :], in_=turned[:].rearrange("p t i -> p i t"))
                else:
                    nc.vector.tensor_copy(out=grouped[:, r, :, :], in_=turned[:].rearrange("p t i -> p i t"))

        regroup_x(0)
        quantise_x(0)
        sort_s()
        regroup_x(1)
        quantise_x(1)
        regroup_x(2)
        for c in range(CHUNKS + Z2_LAG):
            if c == 0:
                product(c, x_codes[c], x_scales[c], out_0, z1_stages, False, False)
            if c < CHUNKS:
                turn_z1(c)
            if 0 < c < CHUNKS:
                product(c, x_codes[c], x_scales[c], out_0, z1_stages, False, False)
            if c >= Z2_LAG:
                d = c - Z2_LAG
                product(d, z1_codes[d], z1_scales[d], out_1, z2_stages, c >= CHUNKS - 1, d == CHUNKS - 1)
            if c + 2 < CHUNKS:
                quantise_x(c + 2)
                quantise_z1(c, 0, TILES)
            elif c < CHUNKS:
                for r in range(TILES):
                    quantise_z1(c, r, 1)
            if c + 3 < CHUNKS:
                regroup_x(c + 3)
